import numpy as np
import ml_dtypes


def mxq(x, axis, fmt="e4m3"):
    dtype, down = {"e4m3": (ml_dtypes.float8_e4m3fn, 7), "e5m2": (ml_dtypes.float8_e5m2, 14)}[fmt]
    v = np.moveaxis(np.asarray(x, np.float32).astype(ml_dtypes.bfloat16).astype(np.float64), axis, -1)
    blocks = v.reshape(v.shape[:-1] + (-1, 32))
    amax = np.abs(blocks).max(-1, keepdims=True)
    byte = np.maximum(np.where(amax > 0, np.frexp(amax)[1] - 1 + 127, 0) - down, 1)
    scale = np.exp2(byte - 127.0)
    codes = (blocks / scale).astype(np.float32).astype(dtype).astype(np.float64)
    return np.moveaxis((codes * scale).reshape(v.shape), -1, axis)


WIDE = False


def mx_kscale(k):
    if not WIDE:
        return np.ones(k)
    levels = np.array([10, -10, 5, -5, 0])
    a = np.random.permutation(np.resize(levels, k // 512 * 4)).reshape(k // 512, 4)
    idx = np.arange(k)
    return np.exp2(a[idx // 512, idx % 128 // 32])


BF16 = ml_dtypes.bfloat16


def bf(x):
    return np.asarray(x, np.float32).astype(BF16)


def f64(x):
    return np.asarray(x).astype(np.float64)


E2M1 = np.array([0.0, 0.5, 1.0, 1.5, 2.0, 3.0, 4.0, 6.0, -0.0, -0.5, -1.0, -1.5, -2.0, -3.0, -4.0, -6.0])


def pack_weight(w, fmt):
    k, n = w.shape
    w = f64(bf(w)).reshape(k // 32, 32, n)
    amax = np.abs(w).max(1)
    if fmt == "e4m3":
        byte = np.frexp(amax)[1] - 1 + 127 - 7
    else:
        mant, ex = np.frexp(amax / 6.0)
        byte = np.where(mant > 0.5, ex, ex - 1) + 127
    byte = np.clip(np.where(amax > 0, byte, 1), 1, 254)
    scaled = (w * np.exp2(127.0 - byte)[:, None, :]).reshape(k, n).astype(np.float32)
    by_word = np.ascontiguousarray(scaled.reshape(k // 512, 128, 4, n).transpose(0, 1, 3, 2))
    if fmt == "e4m3":
        words = by_word.astype(ml_dtypes.float8_e4m3fn).view(np.uint8)
    else:
        c = by_word.astype(ml_dtypes.float4_e2m1fn).view(np.uint8) & 0xF
        words = c[..., 0::2] | (c[..., 1::2] << 4)
    return np.ascontiguousarray(words), np.ascontiguousarray(byte.astype(np.uint8).reshape(k // 512, 16, n))


def unpack_weight(words, scales, fmt):
    g, p, n, _ = words.shape
    if fmt == "e4m3":
        vals = np.ascontiguousarray(words).view(ml_dtypes.float8_e4m3fn).astype(np.float64)
    else:
        nib = np.empty((g, p, n, 4), np.uint8)
        nib[..., 0::2] = words & 0xF
        nib[..., 1::2] = words >> 4
        vals = E2M1[nib]
    vals = vals * np.repeat(np.exp2(scales.astype(np.float64) - 127.0), 8, axis=1)[..., None]
    return vals.transpose(0, 1, 3, 2).reshape(g * 512, n)

def pack4(w):
    words, scales = pack_weight(w, "e2m1")
    return words.reshape(words.shape[0], 128, -1), scales


def unpack4(words, scales):
    return unpack_weight(words.reshape(words.shape[0], 128, -1, 2), scales, "e2m1")


W, M, K, N = 4, 512, 2048, 1024


def setup_inputs():
    s = mx_kscale(K)
    x = bf(np.random.standard_normal((W, M, K)) * s)
    stack = (np.random.standard_normal((W, N, K)) / np.sqrt(W * K) / s).swapaxes(1, 2)
    words, scales = pack4(stack.reshape(-1, N))
    bias = bf(np.random.standard_normal((W, M, N)) / np.sqrt(W))
    return {"x": x, "weight_words": words, "weight_scales": scales, "bias": bias}


def reference(x, weight_words, weight_scales, bias):
    w, m, _ = x.shape
    xq = mxq(f64(x), 2, "e4m3")
    wq = unpack4(weight_words, weight_scales).reshape(W, K, N)
    y = (xq @ wq).sum(0) + f64(bias).sum(0)
    m_per_rank = m // w
    return y.reshape(w, m_per_rank, -1)

@@ -1,0 +1,174 @@
+from contextlib import ExitStack
+
+import concourse.mybir as mybir
+from concourse.masks import make_identity
+
+BF16 = mybir.dt.bfloat16
+F32 = mybir.dt.float32
+I32 = mybir.dt.int32
+U8 = mybir.dt.uint8
+U32 = mybir.dt.uint32
+FP8X4 = mybir.dt.float8_e4m3fn_x4
+FP4X4 = mybir.dt.float4_e2m1fn_x4
+ADD = mybir.AluOpType.add
+
+P = 128
+RANKS, M, K, N = 4, 512, 2048, 1024
+K_PASS = 4 * P
+PASSES = K // K_PASS
+M_TILES = M // P
+N_BANK = 512
+N_BANKS = N // N_BANK
+ROUND_TILES = 2
+ROUNDS = M_TILES // ROUND_TILES
+STEPS = ROUNDS * RANKS
+UNITS = ROUND_TILES * PASSES
+WORDS = K_PASS // 2 // 2
+X_BUFS = 4
+BIAS_FIRST_STEP = 3
+
+FLOPS = 2 * M * N * K * RANKS
+
+
+def tile_gemmrstritonpcie_e_kernel(tc, x, weight_words, weight_scales, bias, out):
+    nc = tc.nc
+    x_rows = x.rearrange("r (p t) k -> r p t k", t=M_TILES)
+    bias_rows = bias.rearrange("r (p t) n -> t p r n", t=M_TILES)
+    out_rows = out.rearrange("w q n -> (w q) n").rearrange("(p t) n -> t p n", t=M_TILES)
+    words_i32 = weight_words.bitcast(I32)
+    scales_i32 = weight_scales.bitcast(I32)
+
+    with ExitStack() as stack:
+        keep = stack.enter_context(tc.tile_pool(name="keep", bufs=1))
+        x_pool = stack.enter_context(tc.tile_pool(name="x", bufs=X_BUFS))
+        work = stack.enter_context(tc.tile_pool(name="work", bufs=2))
+        sums = stack.enter_context(tc.psum_pool(name="sums", bufs=1))
+        flipped = stack.enter_context(tc.psum_pool(name="flipped", bufs=4))
+        stack.enter_context(tc.manual_schedule())
+
+        identity = keep.tile([P, P], F32, name="identity")
+        make_identity(nc, identity[:])
+
+        w_words = [keep.tile([P, PASSES, 2 * N], U8, name="w_words_%d" % r, align_bytes=64) for r in range(RANKS)]
+        w_scales = [keep.tile([P, PASSES, N], U8, name="w_scales_%d" % r, align_bytes=64) for r in range(RANKS)]
+        bias_in = [keep.tile([P, RANKS, N], BF16, name="bias_in_%d" % t) for t in range(M_TILES)]
+        product = [keep.tile([P, N], F32, name="product_%d" % t) for t in range(M_TILES)]
+        result = [keep.tile([P, N], F32, name="result_%d" % t) for t in range(M_TILES)]
+        x_in = {}
+        x_sorted = {}
+        x_codes = {}
+        x_scales = {}
+        x_grouped = {}
+        open_sums = {}
+
+        for r in range(RANKS):
+            nc.vector.memset(w_scales[r][:].rearrange("p c n -> p (c n)").bitcast(I32), 0)
+
+        def load_group(i):
+            if i < STEPS:
+                first_tile = (i // RANKS) * ROUND_TILES
+                x_in[i] = x_pool.tile([P, ROUND_TILES, K], BF16, name="x_in")
+                nc.sync.dma_start(
+                    out=x_in[i][:], in_=x_rows[i % RANKS, :, first_tile : first_tile + ROUND_TILES, :]
+                )
+            if 1 <= i <= RANKS:
+                rank = i - 1
+                groups = slice(rank * PASSES, (rank + 1) * PASSES)
+                nc.sync.dma_start(
+                    out=w_words[rank][:].bitcast(I32), in_=words_i32[groups].rearrange("g p b -> p g b")
+                )
+                rows = scales_i32[groups].rearrange("g (h r) n -> r h g n", r=4)
+                for r in range(4):
+                    nc.sync.dma_start(out=w_scales[rank][:].bitcast(I32)[r:P:32, :, :], in_=rows[r])
+            if i > RANKS:
+                t = i - RANKS - 1
+                nc.sync.dma_start(out=bias_in[t][:], in_=bias_rows[t])
+
+        def sort_words(i):
+            x_sorted[i] = work.tile([P, UNITS, 2, WORDS], F32, name="x_sorted")
+            nc.vector.tensor_copy(
+                out=x_sorted[i][:],
+                in_=x_in[i][:].rearrange("p t k -> p (t k)").bitcast(F32).rearrange(
+                    "p (n w u) -> p n u w", n=UNITS, u=2
+                ),
+            )
+
+        def transpose(i):
+            x_grouped[i] = work.tile([P, UNITS, 4 * P], BF16, name="x_grouped", align_bytes=64)
+            grouped_words = x_grouped[i][:].bitcast(F32).rearrange("p n (m u) -> p n m u", u=2)
+            for n in range(0, UNITS, 2):
+                bank = flipped.tile([P, 2, 2, P], F32, name="bank")
+                for j in range(2):
+                    for u in range(2):
+                        nc.tensor.transpose(bank[:, j, u, :], x_sorted[i][:, n + j, u, :], identity[:])
+                nc.scalar.copy(out=grouped_words[:, n : n + 2, :, :], in_=bank[:].rearrange("p j u m -> p j m u"))
+
+        def quantise(i):
+            x_codes[i] = work.tile([P, UNITS, P], U32, name="x_codes", align_bytes=64)
+            x_scales[i] = work.tile([P, UNITS, P], U8, name="x_scales", align_bytes=64)
+            for t in range(ROUND_TILES):
+                units = slice(t * PASSES, (t + 1) * PASSES)
+                nc.vector.quantize_mx(
+                    out=x_codes[i][:, units, :].rearrange("p n m -> p (n m)").bitcast(FP8X4),
+                    scales=x_scales[i][:, units, :].rearrange("p n m -> p (n m)"),
+                    in_=x_grouped[i][:, units, :].rearrange("p n f -> p (n f)"),
+                )
+
+        def multiply(i):
+            rank = i % RANKS
+            for t in range(ROUND_TILES):
+                for b in range(N_BANKS):
+                    if rank == 0:
+                        open_sums[(t, b)] = sums.tile([P, N_BANK], F32, name="sum_%d_%d" % (t, b))
+                    for c in range(PASSES):
+                        nc.tensor.matmul_mx(
+                            out=open_sums[(t, b)][:],
+                            lhsT=x_codes[i][:, t * PASSES + c, :].bitcast(FP8X4),
+                            lhsT_scale=x_scales[i][:, t * PASSES + c, :],
+                            rhs=w_words[rank][:, c, 2 * N_BANK * b : 2 * N_BANK * (b + 1)].bitcast(FP4X4),
+                            rhs_scale=w_scales[rank][:, c, N_BANK * b : N_BANK * (b + 1)],
+                            start=(rank == 0 and c == 0),
+                            stop=(rank == RANKS - 1 and c == PASSES - 1),
+                        )
+                    if rank == RANKS - 1:
+                        tile_index = (i // RANKS) * ROUND_TILES + t
+                        nc.scalar.copy(
+                            out=product[tile_index][:, N_BANK * b : N_BANK * (b + 1)], in_=open_sums[(t, b)][:]
+                        )
+
+        def sum_bias(t):
+            pair = work.tile([P, 2, N], F32, name="pair")
+            nc.vector.tensor_tensor(out=pair[:], in0=bias_in[t][:, 0:2, :], in1=bias_in[t][:, 2:4, :], op=ADD)
+            nc.vector.tensor_tensor(out=result[t][:], in0=pair[:, 0, :], in1=pair[:, 1, :], op=ADD)
+
+        def add_bias_and_store(t):
+            for b in range(N_BANKS):
+                cols = slice(N_BANK * b, N_BANK * (b + 1))
+                nc.vector.tensor_tensor(out=result[t][:, cols], in0=product[t][:, cols], in1=result[t][:, cols], op=ADD)
+                nc.sync.dma_start(out=out_rows[t][:, cols], in_=result[t][:, cols])
+
+        for i in range(X_BUFS):
+            load_group(i)
+        sort_words(0)
+        load_group(X_BUFS)
+        transpose(0)
+        sort_words(1)
+        load_group(X_BUFS + 1)
+        quantise(0)
+        for i in range(STEPS):
+            if i + 1 < STEPS:
+                transpose(i + 1)
+            if i + 2 < STEPS:
+                sort_words(i + 2)
+            if i + 2 + X_BUFS <= STEPS:
+                load_group(i + 2 + X_BUFS)
+            multiply(i)
+            if i + 1 < STEPS:
+                quantise(i + 1)
+            t = i - BIAS_FIRST_STEP
+            if 0 <= t < M_TILES:
+                sum_bias(t)
+                if t < ROUND_TILES:
+                    add_bias_and_store(t)
+        for t in range(ROUND_TILES, M_TILES):
+            add_bias_and_store(t)

@@ -17,15 +17,14 @@ RANKS, M, K, N = 4, 512, 2048, 1024
 K_PASS = 4 * P
 PASSES = K // K_PASS
 M_TILES = M // P
-N_BANK = 512
-N_BANKS = N // N_BANK
-ROUND_TILES = 2
-ROUNDS = M_TILES // ROUND_TILES
-STEPS = ROUNDS * RANKS
-UNITS = ROUND_TILES * PASSES
-WORDS = K_PASS // 2 // 2
+HALF = 512
+LEFT, RIGHT = 0, 1
+STEP_TILES = 2
+STEPS_PER_RANK = M_TILES // STEP_TILES
+STEPS = RANKS * STEPS_PER_RANK
+UNITS = STEP_TILES * PASSES
+WORDS = K_PASS // 4
 X_BUFS = 4
-BIAS_FIRST_STEP = 3
 
 FLOPS = 2 * M * N * K * RANKS
 
@@ -42,46 +41,53 @@ def tile_gemmrstritonpcie_e_kernel(tc, x, weight_words, weight_scales, bias, out
         keep = stack.enter_context(tc.tile_pool(name="keep", bufs=1))
         x_pool = stack.enter_context(tc.tile_pool(name="x", bufs=X_BUFS))
         work = stack.enter_context(tc.tile_pool(name="work", bufs=2))
-        sums = stack.enter_context(tc.psum_pool(name="sums", bufs=1))
-        flipped = stack.enter_context(tc.psum_pool(name="flipped", bufs=4))
+        left_banks = stack.enter_context(tc.psum_pool(name="left_banks", bufs=1))
+        other_banks = stack.enter_context(tc.psum_pool(name="other_banks", bufs=4))
         stack.enter_context(tc.manual_schedule())
 
         identity = keep.tile([P, P], F32, name="identity")
         make_identity(nc, identity[:])
 
-        w_words = [keep.tile([P, PASSES, 2 * N], U8, name="w_words_%d" % r, align_bytes=64) for r in range(RANKS)]
+        w_words = {}
+        for r in range(RANKS):
+            for h in (LEFT, RIGHT):
+                w_words[(r, h)] = keep.tile([P, PASSES, 2 * HALF], U8, name="w_words_%d_%d" % (r, h), align_bytes=64)
         w_scales = [keep.tile([P, PASSES, N], U8, name="w_scales_%d" % r, align_bytes=64) for r in range(RANKS)]
+        x_codes = [keep.tile([P, UNITS, P], U32, name="x_codes_%d" % i, align_bytes=64) for i in range(STEPS)]
+        x_scales = [keep.tile([P, UNITS, P], U8, name="x_scales_%d" % i, align_bytes=64) for i in range(STEPS)]
         bias_in = [keep.tile([P, RANKS, N], BF16, name="bias_in_%d" % t) for t in range(M_TILES)]
-        product = [keep.tile([P, N], F32, name="product_%d" % t) for t in range(M_TILES)]
         result = [keep.tile([P, N], F32, name="result_%d" % t) for t in range(M_TILES)]
+        left_sums = [left_banks.tile([P, HALF], F32, name="left_sum_%d" % t) for t in range(M_TILES)]
         x_in = {}
         x_sorted = {}
-        x_codes = {}
-        x_scales = {}
         x_grouped = {}
-        open_sums = {}
 
         for r in range(RANKS):
             nc.vector.memset(w_scales[r][:].rearrange("p c n -> p (c n)").bitcast(I32), 0)
 
-        def load_group(i):
-            if i < STEPS:
-                first_tile = (i // RANKS) * ROUND_TILES
-                x_in[i] = x_pool.tile([P, ROUND_TILES, K], BF16, name="x_in")
-                nc.sync.dma_start(
-                    out=x_in[i][:], in_=x_rows[i % RANKS, :, first_tile : first_tile + ROUND_TILES, :]
-                )
-            if 1 <= i <= RANKS:
-                rank = i - 1
+        def load_words(rank, half):
+            groups = slice(rank * PASSES, (rank + 1) * PASSES)
+            nc.sync.dma_start(
+                out=w_words[(rank, half)][:].bitcast(I32),
+                in_=words_i32[groups, :, HALF // 2 * half : HALF // 2 * (half + 1)].rearrange("g p w -> p g w"),
+            )
+
+        def load_step(i):
+            rank = i // STEPS_PER_RANK
+            first_tile = (i % STEPS_PER_RANK) * STEP_TILES
+            x_in[i] = x_pool.tile([P, STEP_TILES, K], BF16, name="x_in")
+            nc.sync.dma_start(out=x_in[i][:], in_=x_rows[rank, :, first_tile : first_tile + STEP_TILES, :])
+            if i % STEPS_PER_RANK == STEPS_PER_RANK - 1:
+                load_words(rank, LEFT)
                 groups = slice(rank * PASSES, (rank + 1) * PASSES)
-                nc.sync.dma_start(
-                    out=w_words[rank][:].bitcast(I32), in_=words_i32[groups].rearrange("g p b -> p g b")
-                )
                 rows = scales_i32[groups].rearrange("g (h r) n -> r h g n", r=4)
                 for r in range(4):
                     nc.sync.dma_start(out=w_scales[rank][:].bitcast(I32)[r:P:32, :, :], in_=rows[r])
-            if i > RANKS:
-                t = i - RANKS - 1
+
+        def load_for_phase_2():
+            for rank in range(RANKS):
+                load_words(rank, RIGHT)
+            for t in range(M_TILES):
                 nc.sync.dma_start(out=bias_in[t][:], in_=bias_rows[t])
 
         def sort_words(i):
@@ -97,78 +103,79 @@ def tile_gemmrstritonpcie_e_kernel(tc, x, weight_words, weight_scales, bias, out
             x_grouped[i] = work.tile([P, UNITS, 4 * P], BF16, name="x_grouped", align_bytes=64)
             grouped_words = x_grouped[i][:].bitcast(F32).rearrange("p n (m u) -> p n m u", u=2)
             for n in range(0, UNITS, 2):
-                bank = flipped.tile([P, 2, 2, P], F32, name="bank")
+                bank = other_banks.tile([P, 2, 2, P], F32, name="bank")
                 for j in range(2):
                     for u in range(2):
                         nc.tensor.transpose(bank[:, j, u, :], x_sorted[i][:, n + j, u, :], identity[:])
                 nc.scalar.copy(out=grouped_words[:, n : n + 2, :, :], in_=bank[:].rearrange("p j u m -> p j m u"))
 
         def quantise(i):
-            x_codes[i] = work.tile([P, UNITS, P], U32, name="x_codes", align_bytes=64)
-            x_scales[i] = work.tile([P, UNITS, P], U8, name="x_scales", align_bytes=64)
-            for t in range(ROUND_TILES):
-                units = slice(t * PASSES, (t + 1) * PASSES)
+            for s in range(STEP_TILES):
+                units = slice(s * PASSES, (s + 1) * PASSES)
                 nc.vector.quantize_mx(
                     out=x_codes[i][:, units, :].rearrange("p n m -> p (n m)").bitcast(FP8X4),
                     scales=x_scales[i][:, units, :].rearrange("p n m -> p (n m)"),
                     in_=x_grouped[i][:, units, :].rearrange("p n f -> p (n f)"),
                 )
 
-        def multiply(i):
-            rank = i % RANKS
-            for t in range(ROUND_TILES):
-                for b in range(N_BANKS):
-                    if rank == 0:
-                        open_sums[(t, b)] = sums.tile([P, N_BANK], F32, name="sum_%d_%d" % (t, b))
-                    for c in range(PASSES):
-                        nc.tensor.matmul_mx(
-                            out=open_sums[(t, b)][:],
-                            lhsT=x_codes[i][:, t * PASSES + c, :].bitcast(FP8X4),
-                            lhsT_scale=x_scales[i][:, t * PASSES + c, :],
-                            rhs=w_words[rank][:, c, 2 * N_BANK * b : 2 * N_BANK * (b + 1)].bitcast(FP4X4),
-                            rhs_scale=w_scales[rank][:, c, N_BANK * b : N_BANK * (b + 1)],
-                            start=(rank == 0 and c == 0),
-                            stop=(rank == RANKS - 1 and c == PASSES - 1),
-                        )
-                    if rank == RANKS - 1:
-                        tile_index = (i // RANKS) * ROUND_TILES + t
-                        nc.scalar.copy(
-                            out=product[tile_index][:, N_BANK * b : N_BANK * (b + 1)], in_=open_sums[(t, b)][:]
-                        )
+        def one_pass(sums, t, rank, c, half):
+            i = rank * STEPS_PER_RANK + t // STEP_TILES
+            unit = (t % STEP_TILES) * PASSES + c
+            nc.tensor.matmul_mx(
+                out=sums[:],
+                lhsT=x_codes[i][:, unit, :].bitcast(FP8X4),
+                lhsT_scale=x_scales[i][:, unit, :],
+                rhs=w_words[(rank, half)][:, c, :].bitcast(FP4X4),
+                rhs_scale=w_scales[rank][:, c, HALF * half : HALF * (half + 1)],
+                start=(rank == 0 and c == 0),
+                stop=(rank == RANKS - 1 and c == PASSES - 1),
+            )
+
+        def multiply_left(i):
+            for s in range(STEP_TILES):
+                t = (i % STEPS_PER_RANK) * STEP_TILES + s
+                for c in range(PASSES):
+                    one_pass(left_sums[t], t, i // STEPS_PER_RANK, c, LEFT)
 
         def sum_bias(t):
             pair = work.tile([P, 2, N], F32, name="pair")
             nc.vector.tensor_tensor(out=pair[:], in0=bias_in[t][:, 0:2, :], in1=bias_in[t][:, 2:4, :], op=ADD)
             nc.vector.tensor_tensor(out=result[t][:], in0=pair[:, 0, :], in1=pair[:, 1, :], op=ADD)
 
-        def add_bias_and_store(t):
-            for b in range(N_BANKS):
-                cols = slice(N_BANK * b, N_BANK * (b + 1))
-                nc.vector.tensor_tensor(out=result[t][:, cols], in0=product[t][:, cols], in1=result[t][:, cols], op=ADD)
-                nc.sync.dma_start(out=out_rows[t][:, cols], in_=result[t][:, cols])
+        def add_bias_and_store(t, half, sums):
+            cols = slice(HALF * half, HALF * (half + 1))
+            nc.vector.tensor_tensor(out=result[t][:, cols], in0=sums[:], in1=result[t][:, cols], op=ADD)
+            nc.sync.dma_start(out=out_rows[t][:, cols], in_=result[t][:, cols])
 
         for i in range(X_BUFS):
-            load_group(i)
+            load_step(i)
         sort_words(0)
-        load_group(X_BUFS)
+        load_step(X_BUFS)
         transpose(0)
         sort_words(1)
-        load_group(X_BUFS + 1)
+        load_step(X_BUFS + 1)
         quantise(0)
         for i in range(STEPS):
             if i + 1 < STEPS:
                 transpose(i + 1)
             if i + 2 < STEPS:
                 sort_words(i + 2)
-            if i + 2 + X_BUFS <= STEPS:
-                load_group(i + 2 + X_BUFS)
-            multiply(i)
+            if i + 2 + X_BUFS < STEPS:
+                load_step(i + 2 + X_BUFS)
+            if i + 2 + X_BUFS == STEPS:
+                load_for_phase_2()
+            multiply_left(i)
             if i + 1 < STEPS:
                 quantise(i + 1)
-            t = i - BIAS_FIRST_STEP
-            if 0 <= t < M_TILES:
-                sum_bias(t)
-                if t < ROUND_TILES:
-                    add_bias_and_store(t)
-        for t in range(ROUND_TILES, M_TILES):
-            add_bias_and_store(t)
+
+        sum_bias(0)
+        add_bias_and_store(0, LEFT, left_sums[0])
+        for t in range(M_TILES):
+            right_sum = other_banks.tile([P, HALF], F32, name="bank")
+            for rank in range(RANKS):
+                for c in range(PASSES):
+                    one_pass(right_sum, t, rank, c, RIGHT)
+            if t + 1 < M_TILES:
+                sum_bias(t + 1)
+                add_bias_and_store(t + 1, LEFT, left_sums[t + 1])
+            add_bias_and_store(t, RIGHT, right_sum)

@@ -87,8 +87,7 @@ def tile_gemmrstritonpcie_e_kernel(tc, x, weight_words, weight_scales, bias, out
         def load_for_phase_2():
             for rank in range(RANKS):
                 load_words(rank, RIGHT)
-            for t in range(M_TILES):
-                nc.sync.dma_start(out=bias_in[t][:], in_=bias_rows[t])
+                nc.sync.dma_start(out=bias_in[rank][:], in_=bias_rows[rank])
 
         def sort_words(i):
             x_sorted[i] = work.tile([P, UNITS, 2, WORDS], F32, name="x_sorted")
@@ -168,14 +167,12 @@ def tile_gemmrstritonpcie_e_kernel(tc, x, weight_words, weight_scales, bias, out
             if i + 1 < STEPS:
                 quantise(i + 1)
 
-        sum_bias(0)
-        add_bias_and_store(0, LEFT, left_sums[0])
-        for t in range(M_TILES):
-            right_sum = other_banks.tile([P, HALF], F32, name="bank")
-            for rank in range(RANKS):
+        right_sums = [other_banks.tile([P, HALF], F32, name="bank") for t in range(M_TILES)]
+        for rank in range(RANKS):
+            for t in range(M_TILES):
                 for c in range(PASSES):
-                    one_pass(right_sum, t, rank, c, RIGHT)
-            if t + 1 < M_TILES:
-                sum_bias(t + 1)
-                add_bias_and_store(t + 1, LEFT, left_sums[t + 1])
-            add_bias_and_store(t, RIGHT, right_sum)
+                    one_pass(right_sums[t], t, rank, c, RIGHT)
+            sum_bias(rank)
+            add_bias_and_store(rank, LEFT, left_sums[rank])
+        for t in range(M_TILES):
+            add_bias_and_store(t, RIGHT, right_sums[t])

@@ -19,12 +19,11 @@ PASSES = K // K_PASS
 M_TILES = M // P
 HALF = 512
 LEFT, RIGHT = 0, 1
-STEP_TILES = 2
-STEPS_PER_RANK = M_TILES // STEP_TILES
-STEPS = RANKS * STEPS_PER_RANK
-UNITS = STEP_TILES * PASSES
+STEPS = [(0, 0, 2), (0, 2, 1), (0, 3, 1)] + [(r, t, 2) for r in range(1, RANKS) for t in range(0, M_TILES, 2)]
 WORDS = K_PASS // 4
 X_BUFS = 4
+
+FINE_STEPS = 3
 
 FLOPS = 2 * M * N * K * RANKS
 
@@ -36,6 +35,7 @@ def tile_gemmrstritonpcie_e_kernel(tc, x, weight_words, weight_scales, bias, out
     out_rows = out.rearrange("w q n -> (w q) n").rearrange("(p t) n -> t p n", t=M_TILES)
     words_i32 = weight_words.bitcast(I32)
     scales_i32 = weight_scales.bitcast(I32)
+    n_steps = len(STEPS)
 
     with ExitStack() as stack:
         keep = stack.enter_context(tc.tile_pool(name="keep", bufs=1))
@@ -53,14 +53,24 @@ def tile_gemmrstritonpcie_e_kernel(tc, x, weight_words, weight_scales, bias, out
             for h in (LEFT, RIGHT):
                 w_words[(r, h)] = keep.tile([P, PASSES, 2 * HALF], U8, name="w_words_%d_%d" % (r, h), align_bytes=64)
         w_scales = [keep.tile([P, PASSES, N], U8, name="w_scales_%d" % r, align_bytes=64) for r in range(RANKS)]
-        x_codes = [keep.tile([P, UNITS, P], U32, name="x_codes_%d" % i, align_bytes=64) for i in range(STEPS)]
-        x_scales = [keep.tile([P, UNITS, P], U8, name="x_scales_%d" % i, align_bytes=64) for i in range(STEPS)]
-        bias_in = [keep.tile([P, RANKS, N], BF16, name="bias_in_%d" % t) for t in range(M_TILES)]
+        x_codes = [
+            keep.tile([P, tiles * PASSES, P], U32, name="x_codes_%d" % i, align_bytes=64)
+            for i, (rank, first, tiles) in enumerate(STEPS)
+        ]
+        x_scales = [
+            keep.tile([P, tiles * PASSES, P], U8, name="x_scales_%d" % i, align_bytes=64)
+            for i, (rank, first, tiles) in enumerate(STEPS)
+        ]
         result = [keep.tile([P, N], F32, name="result_%d" % t) for t in range(M_TILES)]
         left_sums = [left_banks.tile([P, HALF], F32, name="left_sum_%d" % t) for t in range(M_TILES)]
+        where = {}
+        for i, (rank, first, tiles) in enumerate(STEPS):
+            for s in range(tiles):
+                where[(rank, first + s)] = (i, s * PASSES)
         x_in = {}
         x_sorted = {}
         x_grouped = {}
+        bias_in = [keep.tile([P, RANKS, N], BF16, name="bias_in_%d" % t) for t in range(M_TILES)]
 
         for r in range(RANKS):
             nc.vector.memset(w_scales[r][:].rearrange("p c n -> p (c n)").bitcast(I32), 0)
@@ -72,36 +82,38 @@ def tile_gemmrstritonpcie_e_kernel(tc, x, weight_words, weight_scales, bias, out
                 in_=words_i32[groups, :, HALF // 2 * half : HALF // 2 * (half + 1)].rearrange("g p w -> p g w"),
             )
 
-        def load_step(i):
-            rank = i // STEPS_PER_RANK
-            first_tile = (i % STEPS_PER_RANK) * STEP_TILES
-            x_in[i] = x_pool.tile([P, STEP_TILES, K], BF16, name="x_in")
-            nc.sync.dma_start(out=x_in[i][:], in_=x_rows[rank, :, first_tile : first_tile + STEP_TILES, :])
-            if i % STEPS_PER_RANK == STEPS_PER_RANK - 1:
-                load_words(rank, LEFT)
-                groups = slice(rank * PASSES, (rank + 1) * PASSES)
-                rows = scales_i32[groups].rearrange("g (h r) n -> r h g n", r=4)
-                for r in range(4):
-                    nc.sync.dma_start(out=w_scales[rank][:].bitcast(I32)[r:P:32, :, :], in_=rows[r])
+        def load_scales(rank):
+            groups = slice(rank * PASSES, (rank + 1) * PASSES)
+            rows = scales_i32[groups].rearrange("g (h r) n -> r h g n", r=4)
+            for r in range(4):
+                nc.sync.dma_start(out=w_scales[rank][:].bitcast(I32)[r:P:32, :, :], in_=rows[r])
 
-        def load_for_phase_2():
-            for rank in range(RANKS):
-                load_words(rank, RIGHT)
-                nc.sync.dma_start(out=bias_in[rank][:], in_=bias_rows[rank])
+        def load_x(i):
+            rank, first, tiles = STEPS[i]
+            if rank == 0:
+                x_in[i] = keep.tile([P, tiles, K], BF16, name="x_first_%d" % i)
+            else:
+                x_in[i] = x_pool.tile([P, 2, K], BF16, name="x_in")
+            share = 1 if rank == 0 else tiles
+            for s in range(0, tiles, share):
+                nc.sync.dma_start(out=x_in[i][:, s : s + share, :], in_=x_rows[rank, :, first + s : first + s + share, :])
+
+        def load_bias(t):
+            nc.sync.dma_start(out=bias_in[t][:], in_=bias_rows[t])
 
         def sort_words(i):
-            x_sorted[i] = work.tile([P, UNITS, 2, WORDS], F32, name="x_sorted")
-            nc.vector.tensor_copy(
-                out=x_sorted[i][:],
-                in_=x_in[i][:].rearrange("p t k -> p (t k)").bitcast(F32).rearrange(
-                    "p (n w u) -> p n u w", n=UNITS, u=2
-                ),
-            )
+            units = STEPS[i][2] * PASSES
+            x_sorted[i] = work.tile([P, units, 2, WORDS], F32, name="x_sorted")
+            words = x_in[i][:].rearrange("p t k -> p (t k)").bitcast(F32).rearrange("p (n w u) -> p n u w", n=units, u=2)
+            piece = 2 if i < FINE_STEPS else units
+            for n in range(0, units, piece):
+                nc.vector.tensor_copy(out=x_sorted[i][:, n : n + piece], in_=words[:, n : n + piece])
 
         def transpose(i):
-            x_grouped[i] = work.tile([P, UNITS, 4 * P], BF16, name="x_grouped", align_bytes=64)
+            units = STEPS[i][2] * PASSES
+            x_grouped[i] = work.tile([P, units, 4 * P], BF16, name="x_grouped", align_bytes=64)
             grouped_words = x_grouped[i][:].bitcast(F32).rearrange("p n (m u) -> p n m u", u=2)
-            for n in range(0, UNITS, 2):
+            for n in range(0, units, 2):
                 bank = other_banks.tile([P, 2, 2, P], F32, name="bank")
                 for j in range(2):
                     for u in range(2):
@@ -109,7 +121,7 @@ def tile_gemmrstritonpcie_e_kernel(tc, x, weight_words, weight_scales, bias, out
                 nc.scalar.copy(out=grouped_words[:, n : n + 2, :, :], in_=bank[:].rearrange("p j u m -> p j m u"))
 
         def quantise(i):
-            for s in range(STEP_TILES):
+            for s in range(STEPS[i][2]):
                 units = slice(s * PASSES, (s + 1) * PASSES)
                 nc.vector.quantize_mx(
                     out=x_codes[i][:, units, :].rearrange("p n m -> p (n m)").bitcast(FP8X4),
@@ -118,8 +130,8 @@ def tile_gemmrstritonpcie_e_kernel(tc, x, weight_words, weight_scales, bias, out
                 )
 
         def one_pass(sums, t, rank, c, half):
-            i = rank * STEPS_PER_RANK + t // STEP_TILES
-            unit = (t % STEP_TILES) * PASSES + c
+            i, first_unit = where[(rank, t)]
+            unit = first_unit + c
             nc.tensor.matmul_mx(
                 out=sums[:],
                 lhsT=x_codes[i][:, unit, :].bitcast(FP8X4),
@@ -131,10 +143,10 @@ def tile_gemmrstritonpcie_e_kernel(tc, x, weight_words, weight_scales, bias, out
             )
 
         def multiply_left(i):
-            for s in range(STEP_TILES):
-                t = (i % STEPS_PER_RANK) * STEP_TILES + s
+            rank, first, tiles = STEPS[i]
+            for t in range(first, first + tiles):
                 for c in range(PASSES):
-                    one_pass(left_sums[t], t, i // STEPS_PER_RANK, c, LEFT)
+                    one_pass(left_sums[t], t, rank, c, LEFT)
 
         def sum_bias(t):
             pair = work.tile([P, 2, N], F32, name="pair")
@@ -146,25 +158,46 @@ def tile_gemmrstritonpcie_e_kernel(tc, x, weight_words, weight_scales, bias, out
             nc.vector.tensor_tensor(out=result[t][:, cols], in0=sums[:], in1=result[t][:, cols], op=ADD)
             nc.sync.dma_start(out=out_rows[t][:, cols], in_=result[t][:, cols])
 
-        for i in range(X_BUFS):
-            load_step(i)
+        loads = []
+        for i, (rank, first, tiles) in enumerate(STEPS):
+            loads.append(("x", i))
+            if first + tiles == (3 if rank == 0 else M_TILES):
+                loads.append(("weight", rank))
+        issued = [0]
+
+        def next_loads(upto):
+            while issued[0] < len(loads):
+                kind, which = loads[issued[0]]
+                if kind == "x" and which > upto:
+                    return
+                issued[0] += 1
+                if kind == "x":
+                    load_x(which)
+                else:
+                    load_scales(which)
+                    load_words(which, LEFT)
+            if upto >= n_steps and issued[0] == len(loads):
+                issued[0] += 1
+                for rank in range(RANKS):
+                    load_words(rank, RIGHT)
+                    load_bias(rank)
+
+        first_pair = 3
+        ahead = first_pair + X_BUFS
+        next_loads(ahead - 1)
         sort_words(0)
-        load_step(X_BUFS)
         transpose(0)
         sort_words(1)
-        load_step(X_BUFS + 1)
         quantise(0)
-        for i in range(STEPS):
-            if i + 1 < STEPS:
+        for i in range(n_steps):
+            if i + 1 < n_steps:
                 transpose(i + 1)
-            if i + 2 < STEPS:
+            if i + 2 < n_steps:
                 sort_words(i + 2)
-            if i + 2 + X_BUFS < STEPS:
-                load_step(i + 2 + X_BUFS)
-            if i + 2 + X_BUFS == STEPS:
-                load_for_phase_2()
+                if i + 2 >= first_pair:
+                    next_loads(i + 2 + X_BUFS)
             multiply_left(i)
-            if i + 1 < STEPS:
+            if i + 1 < n_steps:
                 quantise(i + 1)
 
         right_sums = [other_banks.tile([P, HALF], F32, name="bank") for t in range(M_TILES)]

@@ -19,11 +19,12 @@ PASSES = K // K_PASS
 M_TILES = M // P
 HALF = 512
 LEFT, RIGHT = 0, 1
-STEPS = [(0, 0, 2), (0, 2, 1), (0, 3, 1)] + [(r, t, 2) for r in range(1, RANKS) for t in range(0, M_TILES, 2)]
+STEPS = [(r, t, 2) for r in range(RANKS) for t in range(0, M_TILES, 2)][:-1] + [(RANKS - 1, 2, 1), (RANKS - 1, 3, 1)]
 WORDS = K_PASS // 4
 X_BUFS = 4
 
-FINE_STEPS = 3
+FINE_STEPS = 2
+EARLY_RIGHT = (0, 1)
 
 FLOPS = 2 * M * N * K * RANKS
 
@@ -68,6 +69,7 @@ def tile_gemmrstritonpcie_e_kernel(tc, x, weight_words, weight_scales, bias, out
             for s in range(tiles):
                 where[(rank, first + s)] = (i, s * PASSES)
         x_in = {}
+        right_sums = {}
         x_sorted = {}
         x_grouped = {}
         bias_in = [keep.tile([P, RANKS, N], BF16, name="bias_in_%d" % t) for t in range(M_TILES)]
@@ -93,8 +95,8 @@ def tile_gemmrstritonpcie_e_kernel(tc, x, weight_words, weight_scales, bias, out
             if rank == 0:
                 x_in[i] = keep.tile([P, tiles, K], BF16, name="x_first_%d" % i)
             else:
-                x_in[i] = x_pool.tile([P, 2, K], BF16, name="x_in")
-            share = 1 if rank == 0 else tiles
+                x_in[i] = x_pool.tile([P, tiles, K], BF16, name="x_in")
+            share = 1 if i == 0 else tiles
             for s in range(0, tiles, share):
                 nc.sync.dma_start(out=x_in[i][:, s : s + share, :], in_=x_rows[rank, :, first + s : first + s + share, :])
 
@@ -105,7 +107,7 @@ def tile_gemmrstritonpcie_e_kernel(tc, x, weight_words, weight_scales, bias, out
             units = STEPS[i][2] * PASSES
             x_sorted[i] = work.tile([P, units, 2, WORDS], F32, name="x_sorted")
             words = x_in[i][:].rearrange("p t k -> p (t k)").bitcast(F32).rearrange("p (n w u) -> p n u w", n=units, u=2)
-            piece = 2 if i < FINE_STEPS else units
+            piece = 2 if i < FINE_STEPS or STEPS[i][2] == 1 else units
             for n in range(0, units, piece):
                 nc.vector.tensor_copy(out=x_sorted[i][:, n : n + piece], in_=words[:, n : n + piece])
 
@@ -148,10 +150,22 @@ def tile_gemmrstritonpcie_e_kernel(tc, x, weight_words, weight_scales, bias, out
                 for c in range(PASSES):
                     one_pass(left_sums[t], t, rank, c, LEFT)
 
+        def multiply_right(rank, row_tiles):
+            for t in row_tiles:
+                if t not in right_sums:
+                    right_sums[t] = other_banks.tile([P, HALF], F32, name="bank")
+                for c in range(PASSES):
+                    one_pass(right_sums[t], t, rank, c, RIGHT)
+
         def sum_bias(t):
             pair = work.tile([P, 2, N], F32, name="pair")
-            nc.vector.tensor_tensor(out=pair[:], in0=bias_in[t][:, 0:2, :], in1=bias_in[t][:, 2:4, :], op=ADD)
-            nc.vector.tensor_tensor(out=result[t][:], in0=pair[:, 0, :], in1=pair[:, 1, :], op=ADD)
+            halves = [slice(HALF * h, HALF * (h + 1)) for h in (LEFT, RIGHT)]
+            for cols in halves:
+                nc.vector.tensor_tensor(
+                    out=pair[:, :, cols], in0=bias_in[t][:, 0:2, cols], in1=bias_in[t][:, 2:4, cols], op=ADD
+                )
+            for cols in halves:
+                nc.vector.tensor_tensor(out=result[t][:, cols], in0=pair[:, 0, cols], in1=pair[:, 1, cols], op=ADD)
 
         def add_bias_and_store(t, half, sums):
             cols = slice(HALF * half, HALF * (half + 1))
@@ -161,7 +175,7 @@ def tile_gemmrstritonpcie_e_kernel(tc, x, weight_words, weight_scales, bias, out
         loads = []
         for i, (rank, first, tiles) in enumerate(STEPS):
             loads.append(("x", i))
-            if first + tiles == (3 if rank == 0 else M_TILES):
+            if first + tiles == (2 if rank == RANKS - 1 else M_TILES):
                 loads.append(("weight", rank))
         issued = [0]
 
@@ -174,15 +188,15 @@ def tile_gemmrstritonpcie_e_kernel(tc, x, weight_words, weight_scales, bias, out
                 if kind == "x":
                     load_x(which)
                 else:
-                    load_scales(which)
                     load_words(which, LEFT)
+                    load_scales(which)
             if upto >= n_steps and issued[0] == len(loads):
                 issued[0] += 1
                 for rank in range(RANKS):
                     load_words(rank, RIGHT)
                     load_bias(rank)
 
-        first_pair = 3
+        first_pair = 2
         ahead = first_pair + X_BUFS
         next_loads(ahead - 1)
         sort_words(0)
@@ -196,15 +210,14 @@ def tile_gemmrstritonpcie_e_kernel(tc, x, weight_words, weight_scales, bias, out
                 sort_words(i + 2)
                 if i + 2 >= first_pair:
                     next_loads(i + 2 + X_BUFS)
+            if i == n_steps - 1:
+                multiply_right(0, EARLY_RIGHT)
             multiply_left(i)
             if i + 1 < n_steps:
                 quantise(i + 1)
 
-        right_sums = [other_banks.tile([P, HALF], F32, name="bank") for t in range(M_TILES)]
         for rank in range(RANKS):
-            for t in range(M_TILES):
-                for c in range(PASSES):
-                    one_pass(right_sums[t], t, rank, c, RIGHT)
+            multiply_right(rank, [t for t in range(M_TILES) if rank > 0 or t not in EARLY_RIGHT])
             sum_bias(rank)
             add_bias_and_store(rank, LEFT, left_sums[rank])
         for t in range(M_TILES):

from contextlib import ExitStack

import concourse.mybir as mybir
from concourse.masks import make_identity

BF16 = mybir.dt.bfloat16
F32 = mybir.dt.float32
I32 = mybir.dt.int32
U8 = mybir.dt.uint8
U32 = mybir.dt.uint32
FP8X4 = mybir.dt.float8_e4m3fn_x4
FP4X4 = mybir.dt.float4_e2m1fn_x4
ADD = mybir.AluOpType.add

P = 128
RANKS, M, K, N = 4, 512, 2048, 1024
K_PASS = 4 * P
PASSES = K // K_PASS
M_TILES = M // P
HALF = 512
LEFT, RIGHT = 0, 1
STEPS = [(r, t, 2) for r in range(RANKS) for t in range(0, M_TILES, 2)][:-1] + [(RANKS - 1, 2, 1), (RANKS - 1, 3, 1)]
WORDS = K_PASS // 4
X_BUFS = 4

FINE_STEPS = 2
EARLY_RIGHT = (0, 1)

FLOPS = 2 * M * N * K * RANKS


def tile_gemmrstritonpcie_e_kernel(tc, x, weight_words, weight_scales, bias, out):
    nc = tc.nc
    x_rows = x.rearrange("r (p t) k -> r p t k", t=M_TILES)
    bias_rows = bias.rearrange("r (p t) n -> t p r n", t=M_TILES)
    out_rows = out.rearrange("w q n -> (w q) n").rearrange("(p t) n -> t p n", t=M_TILES)
    words_i32 = weight_words.bitcast(I32)
    scales_i32 = weight_scales.bitcast(I32)
    n_steps = len(STEPS)

    with ExitStack() as stack:
        keep = stack.enter_context(tc.tile_pool(name="keep", bufs=1))
        x_pool = stack.enter_context(tc.tile_pool(name="x", bufs=X_BUFS))
        work = stack.enter_context(tc.tile_pool(name="work", bufs=2))
        left_banks = stack.enter_context(tc.psum_pool(name="left_banks", bufs=1))
        other_banks = stack.enter_context(tc.psum_pool(name="other_banks", bufs=4))
        stack.enter_context(tc.manual_schedule())

        identity = keep.tile([P, P], F32, name="identity")
        make_identity(nc, identity[:])

        w_words = {}
        for r in range(RANKS):
            for h in (LEFT, RIGHT):
                w_words[(r, h)] = keep.tile([P, PASSES, 2 * HALF], U8, name="w_words_%d_%d" % (r, h), align_bytes=64)
        w_scales = [keep.tile([P, PASSES, N], U8, name="w_scales_%d" % r, align_bytes=64) for r in range(RANKS)]
        x_codes = [
            keep.tile([P, tiles * PASSES, P], U32, name="x_codes_%d" % i, align_bytes=64)
            for i, (rank, first, tiles) in enumerate(STEPS)
        ]
        x_scales = [
            keep.tile([P, tiles * PASSES, P], U8, name="x_scales_%d" % i, align_bytes=64)
            for i, (rank, first, tiles) in enumerate(STEPS)
        ]
        result = [keep.tile([P, N], F32, name="result_%d" % t) for t in range(M_TILES)]
        left_sums = [left_banks.tile([P, HALF], F32, name="left_sum_%d" % t) for t in range(M_TILES)]
        where = {}
        for i, (rank, first, tiles) in enumerate(STEPS):
            for s in range(tiles):
                where[(rank, first + s)] = (i, s * PASSES)
        x_in = {}
        right_sums = {}
        x_sorted = {}
        x_grouped = {}
        bias_in = [keep.tile([P, RANKS, N], BF16, name="bias_in_%d" % t) for t in range(M_TILES)]

        for r in range(RANKS):
            nc.vector.memset(w_scales[r][:].rearrange("p c n -> p (c n)").bitcast(I32), 0)

        def load_words(rank, half):
            groups = slice(rank * PASSES, (rank + 1) * PASSES)
            nc.sync.dma_start(
                out=w_words[(rank, half)][:].bitcast(I32),
                in_=words_i32[groups, :, HALF // 2 * half : HALF // 2 * (half + 1)].rearrange("g p w -> p g w"),
            )

        def load_scales(rank):
            groups = slice(rank * PASSES, (rank + 1) * PASSES)
            rows = scales_i32[groups].rearrange("g (h r) n -> r h g n", r=4)
            for r in range(4):
                nc.sync.dma_start(out=w_scales[rank][:].bitcast(I32)[r:P:32, :, :], in_=rows[r])

        def load_x(i):
            rank, first, tiles = STEPS[i]
            if rank == 0:
                x_in[i] = keep.tile([P, tiles, K], BF16, name="x_first_%d" % i)
            else:
                x_in[i] = x_pool.tile([P, tiles, K], BF16, name="x_in")
            share = 1 if i == 0 else tiles
            for s in range(0, tiles, share):
                nc.sync.dma_start(out=x_in[i][:, s : s + share, :], in_=x_rows[rank, :, first + s : first + s + share, :])

        def load_bias(t):
            nc.sync.dma_start(out=bias_in[t][:], in_=bias_rows[t])

        def sort_words(i):
            units = STEPS[i][2] * PASSES
            x_sorted[i] = work.tile([P, units, 2, WORDS], F32, name="x_sorted")
            words = x_in[i][:].rearrange("p t k -> p (t k)").bitcast(F32).rearrange("p (n w u) -> p n u w", n=units, u=2)
            piece = 2 if i < FINE_STEPS or STEPS[i][2] == 1 else units
            for n in range(0, units, piece):
                nc.vector.tensor_copy(out=x_sorted[i][:, n : n + piece], in_=words[:, n : n + piece])

        def transpose(i):
            units = STEPS[i][2] * PASSES
            x_grouped[i] = work.tile([P, units, 4 * P], BF16, name="x_grouped", align_bytes=64)
            grouped_words = x_grouped[i][:].bitcast(F32).rearrange("p n (m u) -> p n m u", u=2)
            for n in range(0, units, 2):
                bank = other_banks.tile([P, 2, 2, P], F32, name="bank")
                for j in range(2):
                    for u in range(2):
                        nc.tensor.transpose(bank[:, j, u, :], x_sorted[i][:, n + j, u, :], identity[:])
                nc.scalar.copy(out=grouped_words[:, n : n + 2, :, :], in_=bank[:].rearrange("p j u m -> p j m u"))

        def quantise(i):
            for s in range(STEPS[i][2]):
                units = slice(s * PASSES, (s + 1) * PASSES)
                nc.vector.quantize_mx(
                    out=x_codes[i][:, units, :].rearrange("p n m -> p (n m)").bitcast(FP8X4),
                    scales=x_scales[i][:, units, :].rearrange("p n m -> p (n m)"),
                    in_=x_grouped[i][:, units, :].rearrange("p n f -> p (n f)"),
                )

        def one_pass(sums, t, rank, c, half):
            i, first_unit = where[(rank, t)]
            unit = first_unit + c
            nc.tensor.matmul_mx(
                out=sums[:],
                lhsT=x_codes[i][:, unit, :].bitcast(FP8X4),
                lhsT_scale=x_scales[i][:, unit, :],
                rhs=w_words[(rank, half)][:, c, :].bitcast(FP4X4),
                rhs_scale=w_scales[rank][:, c, HALF * half : HALF * (half + 1)],
                start=(rank == 0 and c == 0),
                stop=(rank == RANKS - 1 and c == PASSES - 1),
            )

        def multiply_left(i):
            rank, first, tiles = STEPS[i]
            for t in range(first, first + tiles):
                for c in range(PASSES):
                    one_pass(left_sums[t], t, rank, c, LEFT)

        def multiply_right(rank, row_tiles):
            for t in row_tiles:
                if t not in right_sums:
                    right_sums[t] = other_banks.tile([P, HALF], F32, name="bank")
                for c in range(PASSES):
                    one_pass(right_sums[t], t, rank, c, RIGHT)

        def sum_bias(t):
            pair = work.tile([P, 2, N], F32, name="pair")
            halves = [slice(HALF * h, HALF * (h + 1)) for h in (LEFT, RIGHT)]
            for cols in halves:
                nc.vector.tensor_tensor(
                    out=pair[:, :, cols], in0=bias_in[t][:, 0:2, cols], in1=bias_in[t][:, 2:4, cols], op=ADD
                )
            for cols in halves:
                nc.vector.tensor_tensor(out=result[t][:, cols], in0=pair[:, 0, cols], in1=pair[:, 1, cols], op=ADD)

        def add_bias_and_store(t, half, sums):
            cols = slice(HALF * half, HALF * (half + 1))
            nc.vector.tensor_tensor(out=result[t][:, cols], in0=sums[:], in1=result[t][:, cols], op=ADD)
            nc.sync.dma_start(out=out_rows[t][:, cols], in_=result[t][:, cols])

        loads = []
        for i, (rank, first, tiles) in enumerate(STEPS):
            loads.append(("x", i))
            if first + tiles == (2 if rank == RANKS - 1 else M_TILES):
                loads.append(("weight", rank))
        issued = [0]

        def next_loads(upto):
            while issued[0] < len(loads):
                kind, which = loads[issued[0]]
                if kind == "x" and which > upto:
                    return
                issued[0] += 1
                if kind == "x":
                    load_x(which)
                else:
                    load_words(which, LEFT)
                    load_scales(which)
            if upto >= n_steps and issued[0] == len(loads):
                issued[0] += 1
                for rank in range(RANKS):
                    load_words(rank, RIGHT)
                    load_bias(rank)

        first_pair = 2
        ahead = first_pair + X_BUFS
        next_loads(ahead - 1)
        sort_words(0)
        transpose(0)
        sort_words(1)
        quantise(0)
        for i in range(n_steps):
            if i + 1 < n_steps:
                transpose(i + 1)
            if i + 2 < n_steps:
                sort_words(i + 2)
                if i + 2 >= first_pair:
                    next_loads(i + 2 + X_BUFS)
            if i == n_steps - 1:
                multiply_right(0, EARLY_RIGHT)
            multiply_left(i)
            if i + 1 < n_steps:
                quantise(i + 1)

        for rank in range(RANKS):
            multiply_right(rank, [t for t in range(M_TILES) if rank > 0 or t not in EARLY_RIGHT])
            sum_bias(rank)
            add_bias_and_store(rank, LEFT, left_sums[rank])
        for t in range(M_TILES):
            add_bias_and_store(t, RIGHT, right_sums[t])
